import numpy as np
import ml_dtypes


def mxq(x, axis, fmt="e4m3"):
    dtype, down = {"e4m3": (ml_dtypes.float8_e4m3fn, 7), "e5m2": (ml_dtypes.float8_e5m2, 14)}[fmt]
    v = np.moveaxis(np.asarray(x, np.float32).astype(ml_dtypes.bfloat16).astype(np.float64), axis, -1)
    blocks = v.reshape(v.shape[:-1] + (-1, 32))
    amax = np.abs(blocks).max(-1, keepdims=True)
    byte = np.maximum(np.where(amax > 0, np.frexp(amax)[1] - 1 + 127, 0) - down, 1)
    scale = np.exp2(byte - 127.0)
    codes = (blocks / scale).astype(np.float32).astype(dtype).astype(np.float64)
    return np.moveaxis((codes * scale).reshape(v.shape), -1, axis)


WIDE = False


def mx_kscale(k):
    if not WIDE:
        return np.ones(k)
    levels = np.array([10, -10, 5, -5, 0])
    if k % 512:
        return np.exp2(np.random.permutation(np.resize(levels, k // 32))).repeat(32)
    a = np.empty((k // 512, 16))
    for p in range(k // 512):
        a[p, :8] = np.random.permutation(np.resize(levels, 8))
        for g in range(8):
            far = levels[np.abs(levels - a[p, g]) >= 10]
            a[p, g + 8] = far[np.random.randint(len(far))]
    return np.exp2(a.ravel()).repeat(32)


BF16 = ml_dtypes.bfloat16


def bf(x):
    return np.asarray(x, np.float32).astype(BF16)


def f64(x):
    return np.asarray(x).astype(np.float64)


B, D, ELL = 1024, 1024, 4


def setup_inputs():
    s, t = mx_kscale(D), mx_kscale(D)
    return {"x": bf(np.random.standard_normal((B, D))),
            "phi_j": bf(np.random.standard_normal((B, D)) * 0.7 * t / s),
            "phi_k": bf(np.random.standard_normal((B, D)) * 0.7 * s),
            "w_i": bf(np.random.standard_normal((D, D)) / np.sqrt(D) / t),
            "w_j": bf(np.random.standard_normal((D, D)) / np.sqrt(D) * t[:, None] / s)}


def reference(x, phi_j, phi_k, w_i, w_j):
    x, phi_j, phi_k = f64(x), f64(phi_j), f64(phi_k)
    th = np.tanh(x)
    d1 = 1.0 - th * th
    d2 = -2.0 * th * d1
    jvp_jk = mxq(d1 * phi_k, 1, "e4m3") @ mxq(f64(w_j), 1, "e4m3").T
    u = d2 * phi_k * phi_j + d1 * jvp_jk
    return mxq(u, 1, "e4m3") @ mxq(f64(w_i), 1, "e4m3").T

@@ -1,0 +1,220 @@
+from contextlib import ExitStack
+
+import concourse.mybir as mybir
+from concourse.masks import make_identity
+
+FLOPS = 2 * 2 * 1024 * 1024 * 1024
+
+F32 = mybir.dt.float32
+BF16 = mybir.dt.bfloat16
+U32 = mybir.dt.uint32
+U8 = mybir.dt.uint8
+FP8X4 = mybir.dt.float8_e4m3fn_x4
+ACT = mybir.ActivationFunctionType
+ALU = mybir.AluOpType
+
+P = 128
+PACK = 4
+K_PASS = P * PACK
+ROWS = 1024
+D = 1024
+PASSES = D // K_PASS
+ROW_TILES = ROWS // P
+SLOTS = D // P
+HALVES = 2
+PAIR = 2
+BANK = 512
+N_OUT = 512
+SLOTS_PER_QUANTISE = 4
+
+
+def transpose_rows(nc, bank, rows, ident):
+    words = rows.bitcast(F32)
+    for g in range(PASSES):
+        for h in range(HALVES):
+            src = g * HALVES * P
+            dst = (h * PASSES + g) * P
+            nc.tensor.transpose(bank[:, dst : dst + P], words[:, src + h : src + HALVES * P : HALVES], ident[:])
+
+
+def packed_order(flat):
+    return flat.rearrange("p (c h e) -> p c h e", h=HALVES, e=PAIR)
+
+
+def bank_in_packed_order(bank):
+    return bank[:].bitcast(BF16).rearrange("p (h c e) -> p c h e", h=HALVES, e=PAIR)
+
+
+def tile_inimnetdisc_pa_kernel(tc, x, phi_j, phi_k, w_i, w_j, out):
+    nc = tc.nc
+    with ExitStack() as ctx:
+        const = ctx.enter_context(tc.tile_pool(name="const", bufs=1))
+        inputs = ctx.enter_context(tc.tile_pool(name="inputs", bufs=1))
+        weights = ctx.enter_context(tc.tile_pool(name="weights", bufs=1))
+        wstage = ctx.enter_context(tc.tile_pool(name="wstage", bufs=2))
+        work = ctx.enter_context(tc.tile_pool(name="work", bufs=2))
+        keep = ctx.enter_context(tc.tile_pool(name="keep", bufs=3))
+        mx = ctx.enter_context(tc.tile_pool(name="mx", bufs=3))
+        results = ctx.enter_context(tc.tile_pool(name="results", bufs=3))
+        psum_t = ctx.enter_context(tc.psum_pool(name="psum_t", bufs=4))
+        psum_v = ctx.enter_context(tc.psum_pool(name="psum_v", bufs=2))
+        psum_o = ctx.enter_context(tc.psum_pool(name="psum_o", bufs=2))
+
+        x_rows = x.rearrange("(i p) d -> i p d", p=P)
+        pj_rows = phi_j.rearrange("(i p) d -> i p d", p=P)
+        pk_rows = phi_k.rearrange("(i p) d -> i p d", p=P)
+        out_rows = out.rearrange("(i p) n -> i p n", p=P)
+        wj_rows = w_j.rearrange("(g p h e) d -> g h p e d", p=P, h=HALVES, e=PAIR)
+        wj_view = [wj_rows[g, h] for g in range(PASSES) for h in range(HALVES)]
+        wi_rows = w_i.rearrange("(c e p) d -> c p e d", p=P, e=PAIR)
+        wi_view = [wi_rows[c] for c in range(SLOTS // PAIR)]
+
+        x_sb, pj_sb, pk_sb = [], [], []
+
+        def load_row_tile(i):
+            x_sb.append(inputs.tile([P, D], BF16, name="x%d" % i))
+            pj_sb.append(inputs.tile([P, D], BF16, name="pj%d" % i))
+            pk_sb.append(inputs.tile([P, D], BF16, name="pk%d" % i))
+            nc.sync.dma_start(out=x_sb[i][:], in_=x_rows[i])
+            nc.sync.dma_start(out=pj_sb[i][:], in_=pj_rows[i])
+            nc.sync.dma_start(out=pk_sb[i][:], in_=pk_rows[i])
+
+        def load_weight(view, name):
+            raw = []
+            for c in range(SLOTS // PAIR):
+                raw.append(weights.tile([P, PAIR, D], BF16, name="%s_raw%d" % (name, c)))
+                nc.sync.dma_start(out=raw[c][:], in_=view[c])
+            return raw
+
+        load_row_tile(0)
+        wj_raw = load_weight(wj_view, "wj")
+        load_row_tile(1)
+        wi_raw = load_weight(wi_view, "wi")
+        for i in range(2, ROW_TILES):
+            load_row_tile(i)
+
+        ident = const.tile([P, P], F32)
+        make_identity(nc, ident[:])
+
+        def quantise_weight(raw, name):
+            codes = weights.tile([P, PASSES, D], U32, name="%s_codes" % name, align_bytes=64)
+            scales = weights.tile([P, PASSES, D], U8, name="%s_scales" % name, align_bytes=64)
+            width = SLOTS_PER_QUANTISE * P
+            for first in range(0, SLOTS, SLOTS_PER_QUANTISE):
+                grouped = wstage.tile([P, PASSES * width * PACK], BF16, align_bytes=64)
+                grouped_words = grouped[:].bitcast(F32).rearrange(
+                    "p (g s c h) -> p g s c h", g=PASSES, s=SLOTS_PER_QUANTISE, h=HALVES
+                )
+                for s in range(SLOTS_PER_QUANTISE):
+                    slot = first + s
+                    w_bank = psum_t.tile([P, BANK], F32, tag="bank")
+                    transpose_rows(nc, w_bank, raw[slot // PAIR][:, slot % PAIR, :], ident)
+                    nc.scalar.copy(
+                        out=grouped_words[:, :, s, :, :],
+                        in_=w_bank[:].rearrange("p (h g c) -> p g c h", h=HALVES, g=PASSES),
+                    )
+                for g in range(PASSES):
+                    cols = slice(first * P, first * P + width)
+                    nc.vector.quantize_mx(
+                        out=codes[:, g, cols].bitcast(FP8X4),
+                        scales=scales[:, g, cols],
+                        in_=grouped[:, g * width * PACK : (g + 1) * width * PACK],
+                    )
+            return codes, scales
+
+        d1_of, q_of, g_of, u_of = {}, {}, {}, {}
+
+        def stage_a(i):
+            x_bank = psum_t.tile([P, BANK], F32, tag="bank")
+            transpose_rows(nc, x_bank, x_sb[i][:], ident)
+            pj_bank = psum_t.tile([P, BANK], F32, tag="bank")
+            transpose_rows(nc, pj_bank, pj_sb[i][:], ident)
+            pk_bank = psum_t.tile([P, BANK], F32, tag="bank")
+            transpose_rows(nc, pk_bank, pk_sb[i][:], ident)
+
+            th = work.tile([P, D], F32)
+            nc.scalar.activation(out=packed_order(th[:]), in_=bank_in_packed_order(x_bank), func=ACT.Tanh)
+            sq = work.tile([P, D], F32)
+            nc.scalar.activation(out=sq[:], in_=th[:], func=ACT.Square)
+            d1 = keep.tile([P, D], F32)
+            nc.scalar.activation(out=d1[:], in_=sq[:], func=ACT.Copy, scale=-1.0, bias=1.0)
+
+            tj = work.tile([P, D], F32)
+            nc.vector.tensor_tensor(
+                out=packed_order(tj[:]), in0=packed_order(th[:]), in1=bank_in_packed_order(pj_bank), op=ALU.mult
+            )
+            g_bf = mx.tile([P, D], BF16, align_bytes=64)
+            nc.vector.tensor_tensor(
+                out=packed_order(g_bf[:]), in0=packed_order(d1[:]), in1=bank_in_packed_order(pk_bank), op=ALU.mult
+            )
+            q = keep.tile([P, D], F32)
+            nc.vector.tensor_tensor(
+                out=packed_order(q[:]), in0=packed_order(tj[:]), in1=bank_in_packed_order(pk_bank), op=ALU.mult
+            )
+            g_codes = mx.tile([P, PASSES * P], U32, align_bytes=64)
+            g_scales = mx.tile([P, PASSES * P], U8, align_bytes=64)
+            nc.vector.quantize_mx(out=g_codes[:].bitcast(FP8X4), scales=g_scales[:], in_=g_bf[:])
+            d1_of[i], q_of[i], g_of[i] = d1, q, (g_codes, g_scales)
+
+        def stage_b(i):
+            g_codes, g_scales = g_of[i]
+            d1, q = d1_of[i], q_of[i]
+            s_sum = work.tile([P, D], F32)
+            for g2 in range(PASSES):
+                v_bank = psum_v.tile([P, BANK], F32)
+                for t in range(PACK):
+                    slot = g2 * PACK + t
+                    for g in range(PASSES):
+                        nc.tensor.matmul_mx(
+                            out=v_bank[:, t * P : (t + 1) * P],
+                            lhsT=wj_codes[:, g, slot * P : (slot + 1) * P].bitcast(FP8X4),
+                            lhsT_scale=wj_scales[:, g, slot * P : (slot + 1) * P],
+                            rhs=g_codes[:, g * P : (g + 1) * P].bitcast(FP8X4),
+                            rhs_scale=g_scales[:, g * P : (g + 1) * P],
+                            start=(g == 0),
+                            stop=(g == PASSES - 1),
+                        )
+                part = slice(g2 * K_PASS, (g2 + 1) * K_PASS)
+                nc.vector.scalar_tensor_tensor(
+                    out=s_sum[:, part].rearrange("p (r t) -> p r t", t=PACK),
+                    in0=q[:, part].rearrange("p (r t) -> p r t", t=PACK),
+                    scalar=-2.0,
+                    in1=v_bank[:].rearrange("p (t r) -> p r t", t=PACK),
+                    op0=ALU.mult,
+                    op1=ALU.add,
+                )
+            u_bf = mx.tile([P, D], BF16, align_bytes=64)
+            nc.vector.tensor_tensor(out=u_bf[:], in0=s_sum[:], in1=d1[:], op=ALU.mult)
+            u_codes = mx.tile([P, PASSES * P], U32, align_bytes=64)
+            u_scales = mx.tile([P, PASSES * P], U8, align_bytes=64)
+            nc.vector.quantize_mx(out=u_codes[:].bitcast(FP8X4), scales=u_scales[:], in_=u_bf[:])
+            u_of[i] = (u_codes, u_scales)
+
+        def stage_c(i):
+            u_codes, u_scales = u_of[i]
+            out_sb = results.tile([P, D], F32)
+            for n in range(D // N_OUT):
+                cols = slice(n * N_OUT, (n + 1) * N_OUT)
+                o_bank = psum_o.tile([P, BANK], F32)
+                for g2 in range(PASSES):
+                    nc.tensor.matmul_mx(
+                        out=o_bank[:],
+                        lhsT=u_codes[:, g2 * P : (g2 + 1) * P].bitcast(FP8X4),
+                        lhsT_scale=u_scales[:, g2 * P : (g2 + 1) * P],
+                        rhs=wi_codes[:, g2, cols].bitcast(FP8X4),
+                        rhs_scale=wi_scales[:, g2, cols],
+                        start=(g2 == 0),
+                        stop=(g2 == PASSES - 1),
+                    )
+                nc.scalar.copy(out=out_sb[:, cols], in_=o_bank[:])
+            nc.sync.dma_start(out=out_rows[i], in_=out_sb[:])
+
+        stage_a(0)
+        wj_codes, wj_scales = quantise_weight(wj_raw, "wj")
+        stage_a(1)
+        wi_codes, wi_scales = quantise_weight(wi_raw, "wi")
+        for i in range(ROW_TILES):
+            stage_b(i)
+            if i + 2 < ROW_TILES:
+                stage_a(i + 2)
+            stage_c(i)

@@ -26,6 +26,7 @@ PAIR = 2
 BANK = 512
 N_OUT = 512
 SLOTS_PER_QUANTISE = 4
+FIRST_PRODUCT_TILE = 2
 
 
 def transpose_rows(nc, bank, rows, ident):
@@ -55,6 +56,7 @@ def tile_inimnetdisc_pa_kernel(tc, x, phi_j, phi_k, w_i, w_j, out):
         work = ctx.enter_context(tc.tile_pool(name="work", bufs=2))
         keep = ctx.enter_context(tc.tile_pool(name="keep", bufs=3))
         mx = ctx.enter_context(tc.tile_pool(name="mx", bufs=3))
+        products = ctx.enter_context(tc.tile_pool(name="products", bufs=ROW_TILES - FIRST_PRODUCT_TILE))
         results = ctx.enter_context(tc.tile_pool(name="results", bufs=3))
         psum_t = ctx.enter_context(tc.psum_pool(name="psum_t", bufs=4))
         psum_v = ctx.enter_context(tc.psum_pool(name="psum_v", bufs=2))
@@ -124,11 +126,24 @@ def tile_inimnetdisc_pa_kernel(tc, x, phi_j, phi_k, w_i, w_j, out):
 
         d1_of, q_of, g_of, u_of = {}, {}, {}, {}
 
+        def field_product(i):
+            product = products.tile([P, D], F32)
+            for g in range(PASSES):
+                part = slice(g * K_PASS, (g + 1) * K_PASS)
+                nc.gpsimd.tensor_tensor(
+                    out=product[:, part].rearrange("r (t p) -> r t p", t=PACK),
+                    in0=pj_sb[i][:, part].rearrange("r (p t) -> r t p", t=PACK),
+                    in1=pk_sb[i][:, part].rearrange("r (p t) -> r t p", t=PACK),
+                    op=ALU.mult,
+                )
+            return product
+
         def stage_a(i):
             x_bank = psum_t.tile([P, BANK], F32, tag="bank")
             transpose_rows(nc, x_bank, x_sb[i][:], ident)
-            pj_bank = psum_t.tile([P, BANK], F32, tag="bank")
-            transpose_rows(nc, pj_bank, pj_sb[i][:], ident)
+            if i < FIRST_PRODUCT_TILE:
+                pj_bank = psum_t.tile([P, BANK], F32, tag="bank")
+                transpose_rows(nc, pj_bank, pj_sb[i][:], ident)
             pk_bank = psum_t.tile([P, BANK], F32, tag="bank")
             transpose_rows(nc, pk_bank, pk_sb[i][:], ident)
 
@@ -139,18 +154,34 @@ def tile_inimnetdisc_pa_kernel(tc, x, phi_j, phi_k, w_i, w_j, out):
             d1 = keep.tile([P, D], F32)
             nc.scalar.activation(out=d1[:], in_=sq[:], func=ACT.Copy, scale=-1.0, bias=1.0)
 
-            tj = work.tile([P, D], F32)
-            nc.vector.tensor_tensor(
-                out=packed_order(tj[:]), in0=packed_order(th[:]), in1=bank_in_packed_order(pj_bank), op=ALU.mult
-            )
+            if i < FIRST_PRODUCT_TILE:
+                tj = work.tile([P, D], F32)
+                nc.vector.tensor_tensor(
+                    out=packed_order(tj[:]), in0=packed_order(th[:]), in1=bank_in_packed_order(pj_bank), op=ALU.mult
+                )
             g_bf = mx.tile([P, D], BF16, align_bytes=64)
             nc.vector.tensor_tensor(
                 out=packed_order(g_bf[:]), in0=packed_order(d1[:]), in1=bank_in_packed_order(pk_bank), op=ALU.mult
             )
             q = keep.tile([P, D], F32)
-            nc.vector.tensor_tensor(
-                out=packed_order(q[:]), in0=packed_order(tj[:]), in1=bank_in_packed_order(pk_bank), op=ALU.mult
-            )
+            if i < FIRST_PRODUCT_TILE:
+                nc.vector.tensor_tensor(
+                    out=packed_order(q[:]), in0=packed_order(tj[:]), in1=bank_in_packed_order(pk_bank), op=ALU.mult
+                )
+            else:
+                product = product_of[i]
+                for g in range(PASSES):
+                    part = slice(g * K_PASS, (g + 1) * K_PASS)
+                    p_bank = psum_t.tile([P, BANK], F32, tag="bank")
+                    for t in range(PACK):
+                        cols = slice(g * K_PASS + t * P, g * K_PASS + (t + 1) * P)
+                        nc.tensor.transpose(p_bank[:, t * P : (t + 1) * P], product[:, cols], ident[:])
+                    nc.vector.tensor_tensor(
+                        out=q[:, part].rearrange("p (r t) -> p r t", t=PACK),
+                        in0=th[:, part].rearrange("p (r t) -> p r t", t=PACK),
+                        in1=p_bank[:].rearrange("p (t r) -> p r t", t=PACK),
+                        op=ALU.mult,
+                    )
             g_codes = mx.tile([P, PASSES * P], U32, align_bytes=64)
             g_scales = mx.tile([P, PASSES * P], U8, align_bytes=64)
             nc.vector.quantize_mx(out=g_codes[:].bitcast(FP8X4), scales=g_scales[:], in_=g_bf[:])
@@ -209,6 +240,7 @@ def tile_inimnetdisc_pa_kernel(tc, x, phi_j, phi_k, w_i, w_j, out):
                 nc.scalar.copy(out=out_sb[:, cols], in_=o_bank[:])
             nc.sync.dma_start(out=out_rows[i], in_=out_sb[:])
 
+        product_of = {i: field_product(i) for i in range(FIRST_PRODUCT_TILE, ROW_TILES)}
         stage_a(0)
         wj_codes, wj_scales = quantise_weight(wj_raw, "wj")
         stage_a(1)

@@ -24,9 +24,11 @@ SLOTS = D // P
 HALVES = 2
 PAIR = 2
 BANK = 512
-N_OUT = 512
-SLOTS_PER_QUANTISE = 4
-FIRST_PRODUCT_TILE = 2
+WORDS = D // PACK
+SLOTS_PER_GROUP = 4
+OUT_LAG = SLOTS // SLOTS_PER_GROUP
+WEIGHT_TAGS = ("v0", "v1", "o0", "o1")
+FIELD_STEP = 2
 
 
 def transpose_rows(nc, bank, rows, ident):
@@ -54,13 +56,11 @@ def tile_inimnetdisc_pa_kernel(tc, x, phi_j, phi_k, w_i, w_j, out):
         weights = ctx.enter_context(tc.tile_pool(name="weights", bufs=1))
         wstage = ctx.enter_context(tc.tile_pool(name="wstage", bufs=2))
         work = ctx.enter_context(tc.tile_pool(name="work", bufs=2))
-        keep = ctx.enter_context(tc.tile_pool(name="keep", bufs=3))
+        keep = ctx.enter_context(tc.tile_pool(name="keep", bufs=4))
+        products = ctx.enter_context(tc.tile_pool(name="products", bufs=2))
         mx = ctx.enter_context(tc.tile_pool(name="mx", bufs=3))
-        products = ctx.enter_context(tc.tile_pool(name="products", bufs=ROW_TILES - FIRST_PRODUCT_TILE))
-        results = ctx.enter_context(tc.tile_pool(name="results", bufs=3))
-        psum_t = ctx.enter_context(tc.psum_pool(name="psum_t", bufs=4))
-        psum_v = ctx.enter_context(tc.psum_pool(name="psum_v", bufs=2))
-        psum_o = ctx.enter_context(tc.psum_pool(name="psum_o", bufs=2))
+        results = ctx.enter_context(tc.tile_pool(name="results", bufs=6))
+        psum = ctx.enter_context(tc.psum_pool(name="psum", bufs=1))
 
         x_rows = x.rearrange("(i p) d -> i p d", p=P)
         pj_rows = phi_j.rearrange("(i p) d -> i p d", p=P)
@@ -71,15 +71,20 @@ def tile_inimnetdisc_pa_kernel(tc, x, phi_j, phi_k, w_i, w_j, out):
         wi_rows = w_i.rearrange("(c e p) d -> c p e d", p=P, e=PAIR)
         wi_view = [wi_rows[c] for c in range(SLOTS // PAIR)]
 
-        x_sb, pj_sb, pk_sb = [], [], []
+        ident = const.tile([P, P], F32)
+        make_identity(nc, ident[:])
+
+        x_sb, pj_sb, pk_sb = {}, {}, {}
+        sources = {"x": (x_sb, x_rows), "pk": (pk_sb, pk_rows), "pj": (pj_sb, pj_rows)}
+
+        def load(i, what):
+            tiles, rows = sources[what]
+            tiles[i] = inputs.tile([P, D], BF16, name="%s%d" % (what, i))
+            nc.sync.dma_start(out=tiles[i][:], in_=rows[i])
 
         def load_row_tile(i):
-            x_sb.append(inputs.tile([P, D], BF16, name="x%d" % i))
-            pj_sb.append(inputs.tile([P, D], BF16, name="pj%d" % i))
-            pk_sb.append(inputs.tile([P, D], BF16, name="pk%d" % i))
-            nc.sync.dma_start(out=x_sb[i][:], in_=x_rows[i])
-            nc.sync.dma_start(out=pj_sb[i][:], in_=pj_rows[i])
-            nc.sync.dma_start(out=pk_sb[i][:], in_=pk_rows[i])
+            for what in ("x", "pk", "pj"):
+                load(i, what)
 
         def load_weight(view, name):
             raw = []
@@ -88,165 +93,296 @@ def tile_inimnetdisc_pa_kernel(tc, x, phi_j, phi_k, w_i, w_j, out):
                 nc.sync.dma_start(out=raw[c][:], in_=view[c])
             return raw
 
-        load_row_tile(0)
-        wj_raw = load_weight(wj_view, "wj")
-        load_row_tile(1)
-        wi_raw = load_weight(wi_view, "wi")
-        for i in range(2, ROW_TILES):
-            load_row_tile(i)
-
-        ident = const.tile([P, P], F32)
-        make_identity(nc, ident[:])
-
-        def quantise_weight(raw, name):
+        def packed_weight(name):
             codes = weights.tile([P, PASSES, D], U32, name="%s_codes" % name, align_bytes=64)
             scales = weights.tile([P, PASSES, D], U8, name="%s_scales" % name, align_bytes=64)
-            width = SLOTS_PER_QUANTISE * P
-            for first in range(0, SLOTS, SLOTS_PER_QUANTISE):
-                grouped = wstage.tile([P, PASSES * width * PACK], BF16, align_bytes=64)
-                grouped_words = grouped[:].bitcast(F32).rearrange(
-                    "p (g s c h) -> p g s c h", g=PASSES, s=SLOTS_PER_QUANTISE, h=HALVES
-                )
-                for s in range(SLOTS_PER_QUANTISE):
-                    slot = first + s
-                    w_bank = psum_t.tile([P, BANK], F32, tag="bank")
-                    transpose_rows(nc, w_bank, raw[slot // PAIR][:, slot % PAIR, :], ident)
-                    nc.scalar.copy(
-                        out=grouped_words[:, :, s, :, :],
-                        in_=w_bank[:].rearrange("p (h g c) -> p g c h", h=HALVES, g=PASSES),
-                    )
-                for g in range(PASSES):
-                    cols = slice(first * P, first * P + width)
-                    nc.vector.quantize_mx(
-                        out=codes[:, g, cols].bitcast(FP8X4),
-                        scales=scales[:, g, cols],
-                        in_=grouped[:, g * width * PACK : (g + 1) * width * PACK],
-                    )
             return codes, scales
 
-        d1_of, q_of, g_of, u_of = {}, {}, {}, {}
+        def new_group():
+            return wstage.tile([P, PASSES * SLOTS_PER_GROUP * K_PASS], BF16, name="group", align_bytes=64)
 
-        def field_product(i):
-            product = products.tile([P, D], F32)
+        def weight_slot(raw, group, slot, tag, copy):
+            w_bank = psum.tile([P, BANK], F32, tag=tag, name="w_bank")
+            transpose_rows(nc, w_bank, raw[slot // PAIR][:, slot % PAIR, :], ident)
+            words = group[:].bitcast(F32)
+            words = words.rearrange("p (g s c h) -> p g s c h", g=PASSES, s=SLOTS_PER_GROUP, h=HALVES)
+            copy(out=words[:, :, slot % SLOTS_PER_GROUP, :, :], in_=w_bank[:].rearrange("p (h g c) -> p g c h", h=HALVES, g=PASSES))
+
+        def quantise_slots(packed, group, first):
+            codes, scales = packed
+            cols = slice(first * P, (first + SLOTS_PER_GROUP) * P)
+            width = SLOTS_PER_GROUP * K_PASS
+            for g in range(PASSES):
+                nc.vector.quantize_mx(
+                    out=codes[:, g, cols].bitcast(FP8X4),
+                    scales=scales[:, g, cols],
+                    in_=group[:, g * width : (g + 1) * width],
+                )
+
+        x_bank, pk_bank, p_bank, product = {}, {}, {}, {}
+        th, sq, d1, q, s_sum = {}, {}, {}, {}, {}
+        g_op, u_op, v_bank, o_bank = {}, {}, {}, {}
+
+        def transpose_x(i):
+            x_bank[i] = psum.tile([P, BANK], F32, tag="x", name="x_bank")
+            transpose_rows(nc, x_bank[i], x_sb[i][:], ident)
+
+        def transpose_pk(i):
+            pk_bank[i] = psum.tile([P, BANK], F32, tag="pk", name="pk_bank")
+            transpose_rows(nc, pk_bank[i], pk_sb[i][:], ident)
+
+        def multiply_fields(i):
+            product[i] = products.tile([P, D], F32, name="product")
             for g in range(PASSES):
                 part = slice(g * K_PASS, (g + 1) * K_PASS)
-                nc.gpsimd.tensor_tensor(
-                    out=product[:, part].rearrange("r (t p) -> r t p", t=PACK),
-                    in0=pj_sb[i][:, part].rearrange("r (p t) -> r t p", t=PACK),
-                    in1=pk_sb[i][:, part].rearrange("r (p t) -> r t p", t=PACK),
-                    op=ALU.mult,
-                )
-            return product
+                dst = product[i][:, part].rearrange("r (t p) -> r t p", t=PACK)
+                pj = pj_sb[i][:, part].rearrange("r (p t) -> r t p", t=PACK)
+                pk = pk_sb[i][:, part].rearrange("r (p t) -> r t p", t=PACK)
+                for t in range(0, PACK, FIELD_STEP):
+                    some = slice(t, t + FIELD_STEP)
+                    nc.gpsimd.tensor_tensor(out=dst[:, some], in0=pj[:, some], in1=pk[:, some], op=ALU.mult)
 
-        def stage_a(i):
-            x_bank = psum_t.tile([P, BANK], F32, tag="bank")
-            transpose_rows(nc, x_bank, x_sb[i][:], ident)
-            if i < FIRST_PRODUCT_TILE:
-                pj_bank = psum_t.tile([P, BANK], F32, tag="bank")
-                transpose_rows(nc, pj_bank, pj_sb[i][:], ident)
-            pk_bank = psum_t.tile([P, BANK], F32, tag="bank")
-            transpose_rows(nc, pk_bank, pk_sb[i][:], ident)
+        def transpose_product(i, g):
+            p_bank[i, g] = psum.tile([P, BANK], F32, tag="p%d" % g, name="p_bank")
+            for t in range(PACK):
+                src = g * K_PASS + t * P
+                nc.tensor.transpose(p_bank[i, g][:, t * P : (t + 1) * P], product[i][:, src : src + P], ident[:])
 
-            th = work.tile([P, D], F32)
-            nc.scalar.activation(out=packed_order(th[:]), in_=bank_in_packed_order(x_bank), func=ACT.Tanh)
-            sq = work.tile([P, D], F32)
-            nc.scalar.activation(out=sq[:], in_=th[:], func=ACT.Square)
-            d1 = keep.tile([P, D], F32)
-            nc.scalar.activation(out=d1[:], in_=sq[:], func=ACT.Copy, scale=-1.0, bias=1.0)
+        def tanh_x(i):
+            th[i] = work.tile([P, D], F32, name="th")
+            nc.scalar.activation(out=packed_order(th[i][:]), in_=bank_in_packed_order(x_bank[i]), func=ACT.Tanh)
 
-            if i < FIRST_PRODUCT_TILE:
-                tj = work.tile([P, D], F32)
-                nc.vector.tensor_tensor(
-                    out=packed_order(tj[:]), in0=packed_order(th[:]), in1=bank_in_packed_order(pj_bank), op=ALU.mult
-                )
-            g_bf = mx.tile([P, D], BF16, align_bytes=64)
+        def square_t(i):
+            sq[i] = work.tile([P, D], F32, name="sq")
+            nc.scalar.activation(out=sq[i][:], in_=th[i][:], func=ACT.Square)
+
+        def slope(i):
+            d1[i] = keep.tile([P, D], F32, name="d1")
+            nc.scalar.activation(out=d1[i][:], in_=sq[i][:], func=ACT.Copy, scale=-1.0, bias=1.0)
+
+        def make_g(i, g_bf):
             nc.vector.tensor_tensor(
-                out=packed_order(g_bf[:]), in0=packed_order(d1[:]), in1=bank_in_packed_order(pk_bank), op=ALU.mult
+                out=packed_order(g_bf), in0=packed_order(d1[i][:]), in1=bank_in_packed_order(pk_bank[i]), op=ALU.mult
             )
-            q = keep.tile([P, D], F32)
-            if i < FIRST_PRODUCT_TILE:
-                nc.vector.tensor_tensor(
-                    out=packed_order(q[:]), in0=packed_order(tj[:]), in1=bank_in_packed_order(pk_bank), op=ALU.mult
-                )
-            else:
-                product = product_of[i]
+
+        def make_q(i, g):
+            if g == 0:
+                q[i] = keep.tile([P, D], F32, name="q")
+            part = slice(g * K_PASS, (g + 1) * K_PASS)
+            nc.vector.tensor_tensor(
+                out=q[i][:, part].rearrange("p (r t) -> p r t", t=PACK),
+                in0=th[i][:, part].rearrange("p (r t) -> p r t", t=PACK),
+                in1=p_bank[i, g][:].rearrange("p (t r) -> p r t", t=PACK),
+                op=ALU.mult,
+            )
+
+        def new_operand(count):
+            bf = mx.tile([P, count * D], BF16, tag="bf%d" % count, name="bf", align_bytes=64)
+            codes = mx.tile([P, count * WORDS], U32, tag="codes%d" % count, name="codes", align_bytes=64)
+            scales = mx.tile([P, count * WORDS], U8, tag="scales%d" % count, name="scales", align_bytes=64)
+            return bf, codes, scales
+
+        def quantise(operand, first, count):
+            bf, codes, scales = operand
+            words = slice(first // PACK, (first + count) // PACK)
+            nc.vector.quantize_mx(
+                out=codes[:, words].bitcast(FP8X4), scales=scales[:, words], in_=bf[:, first : first + count]
+            )
+
+        def first_product(i, g2):
+            codes, scales, base = g_op[i]
+            v_bank[i, g2] = psum.tile([P, BANK], F32, tag="v%d" % g2, name="v_bank")
+            for t in range(PACK):
+                slot = slice((g2 * PACK + t) * P, (g2 * PACK + t + 1) * P)
                 for g in range(PASSES):
-                    part = slice(g * K_PASS, (g + 1) * K_PASS)
-                    p_bank = psum_t.tile([P, BANK], F32, tag="bank")
-                    for t in range(PACK):
-                        cols = slice(g * K_PASS + t * P, g * K_PASS + (t + 1) * P)
-                        nc.tensor.transpose(p_bank[:, t * P : (t + 1) * P], product[:, cols], ident[:])
-                    nc.vector.tensor_tensor(
-                        out=q[:, part].rearrange("p (r t) -> p r t", t=PACK),
-                        in0=th[:, part].rearrange("p (r t) -> p r t", t=PACK),
-                        in1=p_bank[:].rearrange("p (t r) -> p r t", t=PACK),
-                        op=ALU.mult,
-                    )
-            g_codes = mx.tile([P, PASSES * P], U32, align_bytes=64)
-            g_scales = mx.tile([P, PASSES * P], U8, align_bytes=64)
-            nc.vector.quantize_mx(out=g_codes[:].bitcast(FP8X4), scales=g_scales[:], in_=g_bf[:])
-            d1_of[i], q_of[i], g_of[i] = d1, q, (g_codes, g_scales)
-
-        def stage_b(i):
-            g_codes, g_scales = g_of[i]
-            d1, q = d1_of[i], q_of[i]
-            s_sum = work.tile([P, D], F32)
-            for g2 in range(PASSES):
-                v_bank = psum_v.tile([P, BANK], F32)
-                for t in range(PACK):
-                    slot = g2 * PACK + t
-                    for g in range(PASSES):
-                        nc.tensor.matmul_mx(
-                            out=v_bank[:, t * P : (t + 1) * P],
-                            lhsT=wj_codes[:, g, slot * P : (slot + 1) * P].bitcast(FP8X4),
-                            lhsT_scale=wj_scales[:, g, slot * P : (slot + 1) * P],
-                            rhs=g_codes[:, g * P : (g + 1) * P].bitcast(FP8X4),
-                            rhs_scale=g_scales[:, g * P : (g + 1) * P],
-                            start=(g == 0),
-                            stop=(g == PASSES - 1),
-                        )
-                part = slice(g2 * K_PASS, (g2 + 1) * K_PASS)
-                nc.vector.scalar_tensor_tensor(
-                    out=s_sum[:, part].rearrange("p (r t) -> p r t", t=PACK),
-                    in0=q[:, part].rearrange("p (r t) -> p r t", t=PACK),
-                    scalar=-2.0,
-                    in1=v_bank[:].rearrange("p (t r) -> p r t", t=PACK),
-                    op0=ALU.mult,
-                    op1=ALU.add,
-                )
-            u_bf = mx.tile([P, D], BF16, align_bytes=64)
-            nc.vector.tensor_tensor(out=u_bf[:], in0=s_sum[:], in1=d1[:], op=ALU.mult)
-            u_codes = mx.tile([P, PASSES * P], U32, align_bytes=64)
-            u_scales = mx.tile([P, PASSES * P], U8, align_bytes=64)
-            nc.vector.quantize_mx(out=u_codes[:].bitcast(FP8X4), scales=u_scales[:], in_=u_bf[:])
-            u_of[i] = (u_codes, u_scales)
-
-        def stage_c(i):
-            u_codes, u_scales = u_of[i]
-            out_sb = results.tile([P, D], F32)
-            for n in range(D // N_OUT):
-                cols = slice(n * N_OUT, (n + 1) * N_OUT)
-                o_bank = psum_o.tile([P, BANK], F32)
-                for g2 in range(PASSES):
+                    rows = slice(base + g * P, base + (g + 1) * P)
                     nc.tensor.matmul_mx(
-                        out=o_bank[:],
-                        lhsT=u_codes[:, g2 * P : (g2 + 1) * P].bitcast(FP8X4),
-                        lhsT_scale=u_scales[:, g2 * P : (g2 + 1) * P],
-                        rhs=wi_codes[:, g2, cols].bitcast(FP8X4),
-                        rhs_scale=wi_scales[:, g2, cols],
-                        start=(g2 == 0),
-                        stop=(g2 == PASSES - 1),
+                        out=v_bank[i, g2][:, t * P : (t + 1) * P],
+                        lhsT=wj[0][:, g, slot].bitcast(FP8X4),
+                        lhsT_scale=wj[1][:, g, slot],
+                        rhs=codes[:, rows].bitcast(FP8X4),
+                        rhs_scale=scales[:, rows],
+                        start=(g == 0),
+                        stop=(g == PASSES - 1),
                     )
-                nc.scalar.copy(out=out_sb[:, cols], in_=o_bank[:])
-            nc.sync.dma_start(out=out_rows[i], in_=out_sb[:])
 
-        product_of = {i: field_product(i) for i in range(FIRST_PRODUCT_TILE, ROW_TILES)}
-        stage_a(0)
-        wj_codes, wj_scales = quantise_weight(wj_raw, "wj")
-        stage_a(1)
-        wi_codes, wi_scales = quantise_weight(wi_raw, "wi")
-        for i in range(ROW_TILES):
-            stage_b(i)
-            if i + 2 < ROW_TILES:
-                stage_a(i + 2)
-            stage_c(i)
+        def add_v(i, g2):
+            if g2 == 0:
+                s_sum[i] = work.tile([P, D], F32, name="s_sum")
+            part = slice(g2 * K_PASS, (g2 + 1) * K_PASS)
+            nc.vector.scalar_tensor_tensor(
+                out=s_sum[i][:, part].rearrange("p (r t) -> p r t", t=PACK),
+                in0=q[i][:, part].rearrange("p (r t) -> p r t", t=PACK),
+                scalar=-2.0,
+                in1=v_bank[i, g2][:].rearrange("p (t r) -> p r t", t=PACK),
+                op0=ALU.mult,
+                op1=ALU.add,
+            )
+
+        def make_u(i, u_bf, part):
+            nc.vector.tensor_tensor(out=u_bf[:, part], in0=s_sum[i][:, part], in1=d1[i][:, part], op=ALU.mult)
+
+        def second_product(i, n, g2):
+            codes, scales = u_op[i]
+            if g2 == 0:
+                o_bank[i, n] = psum.tile([P, BANK], F32, tag="o%d" % n, name="o_bank")
+            rows = slice(g2 * P, (g2 + 1) * P)
+            cols = slice(n * BANK, (n + 1) * BANK)
+            nc.tensor.matmul_mx(
+                out=o_bank[i, n][:],
+                lhsT=codes[:, rows].bitcast(FP8X4),
+                lhsT_scale=scales[:, rows],
+                rhs=wi[0][:, g2, cols].bitcast(FP8X4),
+                rhs_scale=wi[1][:, g2, cols],
+                start=(g2 == 0),
+                stop=(g2 == PASSES - 1),
+            )
+
+        def store_half(i, n, copy):
+            cols = slice(n * BANK, (n + 1) * BANK)
+            half = results.tile([P, BANK], F32, name="half")
+            copy(out=half[:], in_=o_bank[i, n][:])
+            nc.sync.dma_start(out=out_rows[i][:, cols], in_=half[:])
+
+        def second_half(i, n):
+            for g2 in range(PASSES):
+                second_product(i, n, g2)
+
+        def output_rows(i):
+            for n in range(D // BANK):
+                second_half(i, n)
+                store_half(i, n, nc.scalar.copy)
+
+        whole = slice(0, D)
+        with tc.manual_schedule():
+            load(0, "x")
+            load(0, "pk")
+            load(1, "x")
+            load(0, "pj")
+            wj_raw = load_weight(wj_view, "wj")
+            load(1, "pk")
+            load(1, "pj")
+            load_row_tile(2)
+            wi_raw = load_weight(wi_view, "wi")
+            for i in range(3, ROW_TILES):
+                load_row_tile(i)
+            wj, wi = packed_weight("wj"), packed_weight("wi")
+
+            multiply_fields(0)
+            multiply_fields(1)
+            transpose_x(0)
+            tanh_x(0)
+            transpose_pk(0)
+            transpose_x(1)
+            tanh_x(1)
+            square_t(0)
+            group = new_group()
+            for slot in range(0, 3):
+                weight_slot(wj_raw, group, slot, WEIGHT_TAGS[slot % 4], nc.vector.tensor_copy)
+            slope(0)
+            square_t(1)
+            transpose_product(0, 0)
+            transpose_product(0, 1)
+            g0 = new_operand(1)
+            make_g(0, g0[0])
+            slope(1)
+            weight_slot(wj_raw, group, 3, WEIGHT_TAGS[3], nc.vector.tensor_copy)
+            make_q(0, 0)
+            quantise(g0, 0, D)
+            quantise_slots(wj, group, 0)
+            make_q(0, 1)
+            g_op[0] = g0[1], g0[2], 0
+            group = new_group()
+            for slot in range(4, 8):
+                weight_slot(wj_raw, group, slot, WEIGHT_TAGS[slot % 4], nc.scalar.copy)
+            transpose_pk(1)
+            transpose_x(2)
+            transpose_product(1, 0)
+            transpose_product(1, 1)
+            first_product(0, 0)
+            tanh_x(2)
+            square_t(2)
+            g1 = new_operand(1)
+            make_g(1, g1[0])
+            make_q(1, 0)
+            quantise(g1, 0, D)
+            quantise_slots(wj, group, 4)
+            first_product(0, 1)
+            make_q(1, 1)
+            g_op[1] = g1[1], g1[2], 0
+            multiply_fields(2)
+            transpose_pk(2)
+            slope(2)
+            transpose_product(2, 0)
+            transpose_product(2, 1)
+
+            for i in range(ROW_TILES - 2):
+                ahead = i + 3 if i + 3 < ROW_TILES else None
+                if i < OUT_LAG:
+                    group = new_group()
+                    slots = range(i * SLOTS_PER_GROUP, (i + 1) * SLOTS_PER_GROUP)
+                if ahead:
+                    multiply_fields(ahead)
+                if i >= OUT_LAG:
+                    second_half(i - OUT_LAG, 0)
+                if ahead:
+                    transpose_x(ahead)
+                    tanh_x(ahead)
+                if i < OUT_LAG:
+                    for slot in slots[:2]:
+                        weight_slot(wi_raw, group, slot, "o%d" % (slot % 2), nc.scalar.copy)
+                else:
+                    store_half(i - OUT_LAG, 0, nc.scalar.copy)
+                add_v(i, 0)
+                add_v(i, 1)
+                first_product(i + 1, 0)
+                first_product(i + 1, 1)
+                if ahead:
+                    square_t(ahead)
+                pair = new_operand(2)
+                make_g(i + 2, pair[0][:, D : 2 * D])
+                make_u(i, pair[0], whole)
+                if ahead:
+                    transpose_pk(ahead)
+                if i < OUT_LAG:
+                    for slot in slots[2:]:
+                        weight_slot(wi_raw, group, slot, "o%d" % (slot % 2), nc.scalar.copy)
+                else:
+                    second_half(i - OUT_LAG, 1)
+                    store_half(i - OUT_LAG, 1, nc.scalar.copy)
+                if ahead:
+                    slope(ahead)
+                for g in range(PASSES):
+                    make_q(i + 2, g)
+                    if ahead:
+                        transpose_product(ahead, g)
+                quantise(pair, 0, 2 * D)
+                u_op[i] = pair[1][:, 0:WORDS], pair[2][:, 0:WORDS]
+                g_op[i + 2] = pair[1], pair[2], WORDS
+                if i < OUT_LAG:
+                    quantise_slots(wi, group, i * SLOTS_PER_GROUP)
+
+            i = ROW_TILES - 2
+            output_rows(i - 2)
+            add_v(i, 0)
+            add_v(i, 1)
+            first_product(i + 1, 0)
+            first_product(i + 1, 1)
+            output_rows(i - 1)
+            u6 = new_operand(1)
+            make_u(i, u6[0], whole)
+            add_v(i + 1, 0)
+            quantise(u6, 0, D)
+            u_op[i] = u6[1], u6[2]
+            add_v(i + 1, 1)
+            output_rows(i)
+            u7 = new_operand(1)
+            for g2 in range(PASSES):
+                make_u(i + 1, u7[0], slice(g2 * K_PASS, (g2 + 1) * K_PASS))
+            u_op[i + 1] = u7[1], u7[2]
+            for g2 in range(PASSES):
+                quantise(u7, g2 * K_PASS, K_PASS)
+                for n in range(D // BANK):
+                    second_product(i + 1, n, g2)
+            store_half(i + 1, 0, nc.scalar.copy)
+            store_half(i + 1, 1, nc.vector.tensor_copy)

@@ -26,8 +26,9 @@ PAIR = 2
 BANK = 512
 WORDS = D // PACK
 SLOTS_PER_GROUP = 4
-OUT_LAG = SLOTS // SLOTS_PER_GROUP
+ROW_LAYOUT_TILES = 0
 WEIGHT_TAGS = ("v0", "v1", "o0", "o1")
+OUT_TAGS = ("o0", "o1", "x", "pk", "p0", "p1")
 FIELD_STEP = 2
 
 
@@ -56,10 +57,11 @@ def tile_inimnetdisc_pa_kernel(tc, x, phi_j, phi_k, w_i, w_j, out):
         weights = ctx.enter_context(tc.tile_pool(name="weights", bufs=1))
         wstage = ctx.enter_context(tc.tile_pool(name="wstage", bufs=2))
         work = ctx.enter_context(tc.tile_pool(name="work", bufs=2))
+        rowwork = ctx.enter_context(tc.tile_pool(name="rowwork", bufs=1))
         keep = ctx.enter_context(tc.tile_pool(name="keep", bufs=4))
         products = ctx.enter_context(tc.tile_pool(name="products", bufs=2))
         mx = ctx.enter_context(tc.tile_pool(name="mx", bufs=3))
-        results = ctx.enter_context(tc.tile_pool(name="results", bufs=6))
+        results = ctx.enter_context(tc.tile_pool(name="results", bufs=7))
         psum = ctx.enter_context(tc.psum_pool(name="psum", bufs=1))
 
         x_rows = x.rearrange("(i p) d -> i p d", p=P)
@@ -86,11 +88,9 @@ def tile_inimnetdisc_pa_kernel(tc, x, phi_j, phi_k, w_i, w_j, out):
             for what in ("x", "pk", "pj"):
                 load(i, what)
 
-        def load_weight(view, name):
-            raw = []
-            for c in range(SLOTS // PAIR):
-                raw.append(weights.tile([P, PAIR, D], BF16, name="%s_raw%d" % (name, c)))
-                nc.sync.dma_start(out=raw[c][:], in_=view[c])
+        def load_weight(view, name, c):
+            raw = weights.tile([P, PAIR, D], BF16, name="%s_raw%d" % (name, c))
+            nc.sync.dma_start(out=raw[:], in_=view[c])
             return raw
 
         def packed_weight(name):
@@ -121,7 +121,7 @@ def tile_inimnetdisc_pa_kernel(tc, x, phi_j, phi_k, w_i, w_j, out):
 
         x_bank, pk_bank, p_bank, product = {}, {}, {}, {}
         th, sq, d1, q, s_sum = {}, {}, {}, {}, {}
-        g_op, u_op, v_bank, o_bank = {}, {}, {}, {}
+        g_op, u_op, v_bank, o_bank, g_rows, u_rows = {}, {}, {}, {}, {}, {}
 
         def transpose_x(i):
             x_bank[i] = psum.tile([P, BANK], F32, tag="x", name="x_bank")
@@ -140,7 +140,8 @@ def tile_inimnetdisc_pa_kernel(tc, x, phi_j, phi_k, w_i, w_j, out):
                 pk = pk_sb[i][:, part].rearrange("r (p t) -> r t p", t=PACK)
                 for t in range(0, PACK, FIELD_STEP):
                     some = slice(t, t + FIELD_STEP)
-                    nc.gpsimd.tensor_tensor(out=dst[:, some], in0=pj[:, some], in1=pk[:, some], op=ALU.mult)
+                    engine = nc.vector if i == 0 else nc.gpsimd
+                    engine.tensor_tensor(out=dst[:, some], in0=pj[:, some], in1=pk[:, some], op=ALU.mult)
 
         def transpose_product(i, g):
             p_bank[i, g] = psum.tile([P, BANK], F32, tag="p%d" % g, name="p_bank")
@@ -150,15 +151,45 @@ def tile_inimnetdisc_pa_kernel(tc, x, phi_j, phi_k, w_i, w_j, out):
 
         def tanh_x(i):
             th[i] = work.tile([P, D], F32, name="th")
-            nc.scalar.activation(out=packed_order(th[i][:]), in_=bank_in_packed_order(x_bank[i]), func=ACT.Tanh)
+            if i < ROW_LAYOUT_TILES:
+                nc.scalar.activation(out=th[i][:], in_=x_sb[i][:], func=ACT.Tanh)
+            else:
+                nc.scalar.activation(out=packed_order(th[i][:]), in_=bank_in_packed_order(x_bank[i]), func=ACT.Tanh)
 
         def square_t(i):
-            sq[i] = work.tile([P, D], F32, name="sq")
+            pool = keep if i < ROW_LAYOUT_TILES else work
+            sq[i] = pool.tile([P, D], F32, name="d1" if i < ROW_LAYOUT_TILES else "sq")
             nc.scalar.activation(out=sq[i][:], in_=th[i][:], func=ACT.Square)
 
         def slope(i):
             d1[i] = keep.tile([P, D], F32, name="d1")
             nc.scalar.activation(out=d1[i][:], in_=sq[i][:], func=ACT.Copy, scale=-1.0, bias=1.0)
+
+        def rows_fields(i):
+            product[i] = rowwork.tile([P, D], F32, name="row_product")
+            nc.vector.tensor_tensor(out=product[i][:], in0=pj_sb[i][:], in1=pk_sb[i][:], op=ALU.mult)
+
+        def rows_q(i):
+            q[i] = keep.tile([P, D], F32, name="q")
+            nc.vector.tensor_tensor(out=q[i][:], in0=th[i][:], in1=product[i][:], op=ALU.mult)
+
+        def rows_g(i):
+            g_rows[i] = rowwork.tile([P, D], BF16, name="g_rows")
+            nc.vector.scalar_tensor_tensor(
+                out=g_rows[i][:], in0=sq[i][:], scalar=1.0, in1=pk_sb[i][:], op0=ALU.subtract, op1=ALU.mult
+            )
+
+        def rows_u(i):
+            u_rows[i] = rowwork.tile([P, D], BF16, name="u_rows")
+            nc.vector.scalar_tensor_tensor(
+                out=u_rows[i][:], in0=sq[i][:], scalar=1.0, in1=s_sum[i][:], op0=ALU.subtract, op1=ALU.mult
+            )
+
+        def turn_rows(rows, tag, bf):
+            bank = psum.tile([P, BANK], F32, tag=tag, name="turn_bank")
+            transpose_rows(nc, bank, rows, ident)
+            words = bf.bitcast(F32).rearrange("p (g c h) -> p g c h", g=PASSES, h=HALVES)
+            nc.scalar.copy(out=words, in_=bank[:].rearrange("p (h g c) -> p g c h", h=HALVES, g=PASSES))
 
         def make_g(i, g_bf):
             nc.vector.tensor_tensor(
@@ -177,9 +208,10 @@ def tile_inimnetdisc_pa_kernel(tc, x, phi_j, phi_k, w_i, w_j, out):
             )
 
         def new_operand(count):
-            bf = mx.tile([P, count * D], BF16, tag="bf%d" % count, name="bf", align_bytes=64)
-            codes = mx.tile([P, count * WORDS], U32, tag="codes%d" % count, name="codes", align_bytes=64)
-            scales = mx.tile([P, count * WORDS], U8, tag="scales%d" % count, name="scales", align_bytes=64)
+            bf = mx.tile([P, count * D], BF16, tag="bf%d" % count, name="bf", align_bytes=64, bufs=count + 1)
+            live = 2 if count == 1 else ROW_TILES - 2
+            codes = mx.tile([P, count * WORDS], U32, tag="codes%d" % count, name="codes", align_bytes=64, bufs=live)
+            scales = mx.tile([P, count * WORDS], U8, tag="scales%d" % count, name="scales", align_bytes=64, bufs=live)
             return bf, codes, scales
 
         def quantise(operand, first, count):
@@ -192,6 +224,20 @@ def tile_inimnetdisc_pa_kernel(tc, x, phi_j, phi_k, w_i, w_j, out):
         def first_product(i, g2):
             codes, scales, base = g_op[i]
             v_bank[i, g2] = psum.tile([P, BANK], F32, tag="v%d" % g2, name="v_bank")
+            if i < ROW_LAYOUT_TILES:
+                cols = slice(g2 * BANK, (g2 + 1) * BANK)
+                for g in range(PASSES):
+                    rows = slice(base + g * P, base + (g + 1) * P)
+                    nc.tensor.matmul_mx(
+                        out=v_bank[i, g2][:],
+                        lhsT=codes[:, rows].bitcast(FP8X4),
+                        lhsT_scale=scales[:, rows],
+                        rhs=wj[0][:, g, cols].bitcast(FP8X4),
+                        rhs_scale=wj[1][:, g, cols],
+                        start=(g == 0),
+                        stop=(g == PASSES - 1),
+                    )
+                return
             for t in range(PACK):
                 slot = slice((g2 * PACK + t) * P, (g2 * PACK + t + 1) * P)
                 for g in range(PASSES):
@@ -213,7 +259,7 @@ def tile_inimnetdisc_pa_kernel(tc, x, phi_j, phi_k, w_i, w_j, out):
             nc.vector.scalar_tensor_tensor(
                 out=s_sum[i][:, part].rearrange("p (r t) -> p r t", t=PACK),
                 in0=q[i][:, part].rearrange("p (r t) -> p r t", t=PACK),
-                scalar=-2.0,
+                scalar=2.0 if i < ROW_LAYOUT_TILES else -2.0,
                 in1=v_bank[i, g2][:].rearrange("p (t r) -> p r t", t=PACK),
                 op0=ALU.mult,
                 op1=ALU.add,
@@ -224,8 +270,8 @@ def tile_inimnetdisc_pa_kernel(tc, x, phi_j, phi_k, w_i, w_j, out):
 
         def second_product(i, n, g2):
             codes, scales = u_op[i]
-            if g2 == 0:
-                o_bank[i, n] = psum.tile([P, BANK], F32, tag="o%d" % n, name="o_bank")
+            if g2 == 0 and (i, n) not in o_bank:
+                o_bank[i, n] = psum.tile([P, BANK], F32, tag=OUT_TAGS[(HALVES * i + n) % len(OUT_TAGS) if i > 3 else n], name="o_bank")
             rows = slice(g2 * P, (g2 + 1) * P)
             cols = slice(n * BANK, (n + 1) * BANK)
             nc.tensor.matmul_mx(
@@ -255,122 +301,131 @@ def tile_inimnetdisc_pa_kernel(tc, x, phi_j, phi_k, w_i, w_j, out):
 
         whole = slice(0, D)
         with tc.manual_schedule():
-            load(0, "x")
-            load(0, "pk")
-            load(1, "x")
-            load(0, "pj")
-            wj_raw = load_weight(wj_view, "wj")
-            load(1, "pk")
-            load(1, "pj")
+            wj_raw, wi_raw = [], []
+            load_row_tile(0)
+            wj_raw += [load_weight(wj_view, "wj", 0), load_weight(wj_view, "wj", 1)]
+            load_row_tile(1)
+            wj_raw += [load_weight(wj_view, "wj", 2), load_weight(wj_view, "wj", 3)]
             load_row_tile(2)
-            wi_raw = load_weight(wi_view, "wi")
-            for i in range(3, ROW_TILES):
+            load_row_tile(3)
+            wi_raw += [load_weight(wi_view, "wi", c) for c in range(SLOTS // PAIR)]
+            for i in range(4, ROW_TILES):
                 load_row_tile(i)
             wj, wi = packed_weight("wj"), packed_weight("wi")
 
-            multiply_fields(0)
-            multiply_fields(1)
+            first = new_operand(1), new_operand(1)
+            group_a, group_b = new_group(), new_group()
             transpose_x(0)
             tanh_x(0)
             transpose_pk(0)
-            transpose_x(1)
-            tanh_x(1)
+            multiply_fields(0)
             square_t(0)
-            group = new_group()
-            for slot in range(0, 3):
-                weight_slot(wj_raw, group, slot, WEIGHT_TAGS[slot % 4], nc.vector.tensor_copy)
+            weight_slot(wj_raw, group_a, 0, WEIGHT_TAGS[0], nc.vector.tensor_copy)
+            weight_slot(wj_raw, group_a, 1, WEIGHT_TAGS[1], nc.vector.tensor_copy)
             slope(0)
-            square_t(1)
             transpose_product(0, 0)
             transpose_product(0, 1)
-            g0 = new_operand(1)
-            make_g(0, g0[0])
-            slope(1)
-            weight_slot(wj_raw, group, 3, WEIGHT_TAGS[3], nc.vector.tensor_copy)
+            weight_slot(wj_raw, group_a, 2, WEIGHT_TAGS[2], nc.vector.tensor_copy)
+            weight_slot(wj_raw, group_a, 3, WEIGHT_TAGS[3], nc.vector.tensor_copy)
+            transpose_x(1)
+            tanh_x(1)
+            multiply_fields(1)
+            make_g(0, first[0][0][:])
+            square_t(1)
             make_q(0, 0)
-            quantise(g0, 0, D)
-            quantise_slots(wj, group, 0)
             make_q(0, 1)
-            g_op[0] = g0[1], g0[2], 0
-            group = new_group()
-            for slot in range(4, 8):
-                weight_slot(wj_raw, group, slot, WEIGHT_TAGS[slot % 4], nc.scalar.copy)
+            quantise(first[0], 0, D)
             transpose_pk(1)
+            slope(1)
+            for slot in (4, 5):
+                weight_slot(wj_raw, group_b, slot, WEIGHT_TAGS[slot % 4], nc.scalar.copy)
+            quantise_slots(wj, group_a, 0)
             transpose_x(2)
+            for slot in (6, 7):
+                weight_slot(wj_raw, group_b, slot, WEIGHT_TAGS[slot % 4], nc.scalar.copy)
+            tanh_x(2)
             transpose_product(1, 0)
             transpose_product(1, 1)
-            first_product(0, 0)
-            tanh_x(2)
-            square_t(2)
-            g1 = new_operand(1)
-            make_g(1, g1[0])
-            make_q(1, 0)
-            quantise(g1, 0, D)
-            quantise_slots(wj, group, 4)
-            first_product(0, 1)
-            make_q(1, 1)
-            g_op[1] = g1[1], g1[2], 0
-            multiply_fields(2)
+            make_g(1, first[1][0][:])
             transpose_pk(2)
+            multiply_fields(2)
+            g_op[0] = first[0][1], first[0][2], 0
+            g_op[1] = first[1][1], first[1][2], 0
+            first_product(0, 0)
+            make_q(1, 0)
+            make_q(1, 1)
+            square_t(2)
+            quantise_slots(wj, group_b, 4)
+            first_product(0, 1)
+            quantise(first[1], 0, D)
             slope(2)
             transpose_product(2, 0)
             transpose_product(2, 1)
+            transpose_x(3)
 
+            outs = {3: (0,), 4: (1,), 5: (2, 3)}
+            slots_of = {0: (0, 1, 2), 1: (3, 4, 5), 2: (6, 7)}
+            groups = {}
             for i in range(ROW_TILES - 2):
+                j = i + 2
                 ahead = i + 3 if i + 3 < ROW_TILES else None
-                if i < OUT_LAG:
-                    group = new_group()
-                    slots = range(i * SLOTS_PER_GROUP, (i + 1) * SLOTS_PER_GROUP)
+                slots = slots_of.get(i, ())
+                now = outs.get(i, ())
+                pair = new_operand(2)
                 if ahead:
                     multiply_fields(ahead)
-                if i >= OUT_LAG:
-                    second_half(i - OUT_LAG, 0)
-                if ahead:
-                    transpose_x(ahead)
                     tanh_x(ahead)
-                if i < OUT_LAG:
-                    for slot in slots[:2]:
-                        weight_slot(wi_raw, group, slot, "o%d" % (slot % 2), nc.scalar.copy)
-                else:
-                    store_half(i - OUT_LAG, 0, nc.scalar.copy)
                 add_v(i, 0)
                 add_v(i, 1)
+                for s in slots[:2]:
+                    if s % SLOTS_PER_GROUP == 0:
+                        groups[s // SLOTS_PER_GROUP] = new_group()
+                    weight_slot(wi_raw, groups[s // SLOTS_PER_GROUP], s, "o%d" % (s % 2), nc.scalar.copy)
+                for late in now[:1]:
+                    second_half(late, 0)
+                    store_half(late, 0, nc.scalar.copy)
+                if ahead:
+                    square_t(ahead)
                 first_product(i + 1, 0)
                 first_product(i + 1, 1)
                 if ahead:
-                    square_t(ahead)
-                pair = new_operand(2)
-                make_g(i + 2, pair[0][:, D : 2 * D])
+                    slope(ahead)
+                make_g(j, pair[0][:, D : 2 * D])
                 make_u(i, pair[0], whole)
                 if ahead:
                     transpose_pk(ahead)
-                if i < OUT_LAG:
-                    for slot in slots[2:]:
-                        weight_slot(wi_raw, group, slot, "o%d" % (slot % 2), nc.scalar.copy)
-                else:
-                    second_half(i - OUT_LAG, 1)
-                    store_half(i - OUT_LAG, 1, nc.scalar.copy)
-                if ahead:
-                    slope(ahead)
+                for s in slots[2:]:
+                    if s % SLOTS_PER_GROUP == 0:
+                        groups[s // SLOTS_PER_GROUP] = new_group()
+                    weight_slot(wi_raw, groups[s // SLOTS_PER_GROUP], s, "o%d" % (s % 2), nc.scalar.copy)
+                for late in now[:1]:
+                    second_half(late, 1)
+                    store_half(late, 1, nc.scalar.copy)
+                if i + 4 < ROW_TILES:
+                    transpose_x(i + 4)
                 for g in range(PASSES):
-                    make_q(i + 2, g)
+                    make_q(j, g)
                     if ahead:
                         transpose_product(ahead, g)
+                for late in now[1:]:
+                    for n in range(D // BANK):
+                        second_half(late, n)
+                        store_half(late, n, nc.scalar.copy)
                 quantise(pair, 0, 2 * D)
+                for group in {1: (0,), 2: (1,)}.get(i, ()):
+                    quantise_slots(wi, groups[group], group * SLOTS_PER_GROUP)
                 u_op[i] = pair[1][:, 0:WORDS], pair[2][:, 0:WORDS]
-                g_op[i + 2] = pair[1], pair[2], WORDS
-                if i < OUT_LAG:
-                    quantise_slots(wi, group, i * SLOTS_PER_GROUP)
+                g_op[j] = pair[1], pair[2], WORDS
 
             i = ROW_TILES - 2
-            output_rows(i - 2)
             add_v(i, 0)
             add_v(i, 1)
             first_product(i + 1, 0)
             first_product(i + 1, 1)
-            output_rows(i - 1)
+            output_rows(i - 2)
             u6 = new_operand(1)
             make_u(i, u6[0], whole)
+            output_rows(i - 1)
             add_v(i + 1, 0)
             quantise(u6, 0, D)
             u_op[i] = u6[1], u6[2]
@@ -380,6 +435,8 @@ def tile_inimnetdisc_pa_kernel(tc, x, phi_j, phi_k, w_i, w_j, out):
             for g2 in range(PASSES):
                 make_u(i + 1, u7[0], slice(g2 * K_PASS, (g2 + 1) * K_PASS))
             u_op[i + 1] = u7[1], u7[2]
+            for n in range(D // BANK):
+                o_bank[i + 1, n] = psum.tile([P, BANK], F32, tag="v%d" % n, name="o_bank")
             for g2 in range(PASSES):
                 quantise(u7, g2 * K_PASS, K_PASS)
                 for n in range(D // BANK):

@@ -303,8 +303,10 @@ def tile_inimnetdisc_pa_kernel(tc, x, phi_j, phi_k, w_i, w_j, out):
         with tc.manual_schedule():
             wj_raw, wi_raw = [], []
             load_row_tile(0)
+            load(1, "x")
             wj_raw += [load_weight(wj_view, "wj", 0), load_weight(wj_view, "wj", 1)]
-            load_row_tile(1)
+            load(1, "pk")
+            load(1, "pj")
             wj_raw += [load_weight(wj_view, "wj", 2), load_weight(wj_view, "wj", 3)]
             load_row_tile(2)
             load_row_tile(3)
@@ -319,35 +321,36 @@ def tile_inimnetdisc_pa_kernel(tc, x, phi_j, phi_k, w_i, w_j, out):
             tanh_x(0)
             transpose_pk(0)
             multiply_fields(0)
+            transpose_product(0, 0)
+            transpose_product(0, 1)
             square_t(0)
+            transpose_x(1)
+            tanh_x(1)
+            make_q(0, 0)
+            make_q(0, 1)
             weight_slot(wj_raw, group_a, 0, WEIGHT_TAGS[0], nc.vector.tensor_copy)
             weight_slot(wj_raw, group_a, 1, WEIGHT_TAGS[1], nc.vector.tensor_copy)
             slope(0)
-            transpose_product(0, 0)
-            transpose_product(0, 1)
+            square_t(1)
+            slope(1)
+            multiply_fields(1)
             weight_slot(wj_raw, group_a, 2, WEIGHT_TAGS[2], nc.vector.tensor_copy)
             weight_slot(wj_raw, group_a, 3, WEIGHT_TAGS[3], nc.vector.tensor_copy)
-            transpose_x(1)
-            tanh_x(1)
-            multiply_fields(1)
             make_g(0, first[0][0][:])
-            square_t(1)
-            make_q(0, 0)
-            make_q(0, 1)
             quantise(first[0], 0, D)
-            transpose_pk(1)
-            slope(1)
             for slot in (4, 5):
                 weight_slot(wj_raw, group_b, slot, WEIGHT_TAGS[slot % 4], nc.scalar.copy)
             quantise_slots(wj, group_a, 0)
-            transpose_x(2)
             for slot in (6, 7):
                 weight_slot(wj_raw, group_b, slot, WEIGHT_TAGS[slot % 4], nc.scalar.copy)
+            transpose_pk(1)
+            transpose_x(2)
             tanh_x(2)
             transpose_product(1, 0)
             transpose_product(1, 1)
             make_g(1, first[1][0][:])
             transpose_pk(2)
+            transpose_x(3)
             multiply_fields(2)
             g_op[0] = first[0][1], first[0][2], 0
             g_op[1] = first[1][1], first[1][2], 0
@@ -361,7 +364,6 @@ def tile_inimnetdisc_pa_kernel(tc, x, phi_j, phi_k, w_i, w_j, out):
             slope(2)
             transpose_product(2, 0)
             transpose_product(2, 1)
-            transpose_x(3)
 
             outs = {3: (0,), 4: (1,), 5: (2, 3)}
             slots_of = {0: (0, 1, 2), 1: (3, 4, 5), 2: (6, 7)}

@@ -26,7 +26,6 @@ PAIR = 2
 BANK = 512
 WORDS = D // PACK
 SLOTS_PER_GROUP = 4
-ROW_LAYOUT_TILES = 0
 WEIGHT_TAGS = ("v0", "v1", "o0", "o1")
 OUT_TAGS = ("o0", "o1", "x", "pk", "p0", "p1")
 FIELD_STEP = 2
@@ -57,7 +56,6 @@ def tile_inimnetdisc_pa_kernel(tc, x, phi_j, phi_k, w_i, w_j, out):
         weights = ctx.enter_context(tc.tile_pool(name="weights", bufs=1))
         wstage = ctx.enter_context(tc.tile_pool(name="wstage", bufs=2))
         work = ctx.enter_context(tc.tile_pool(name="work", bufs=2))
-        rowwork = ctx.enter_context(tc.tile_pool(name="rowwork", bufs=1))
         keep = ctx.enter_context(tc.tile_pool(name="keep", bufs=4))
         products = ctx.enter_context(tc.tile_pool(name="products", bufs=2))
         mx = ctx.enter_context(tc.tile_pool(name="mx", bufs=3))
@@ -94,8 +92,9 @@ def tile_inimnetdisc_pa_kernel(tc, x, phi_j, phi_k, w_i, w_j, out):
             return raw
 
         def packed_weight(name):
-            codes = weights.tile([P, PASSES, D], U32, name="%s_codes" % name, align_bytes=64)
-            scales = weights.tile([P, PASSES, D], U8, name="%s_scales" % name, align_bytes=64)
+            shape = [P, SLOTS // SLOTS_PER_GROUP, PASSES * SLOTS_PER_GROUP * P]
+            codes = weights.tile(shape, U32, name="%s_codes" % name, align_bytes=64)
+            scales = weights.tile(shape, U8, name="%s_scales" % name, align_bytes=64)
             return codes, scales
 
         def new_group():
@@ -110,18 +109,18 @@ def tile_inimnetdisc_pa_kernel(tc, x, phi_j, phi_k, w_i, w_j, out):
 
         def quantise_slots(packed, group, first):
             codes, scales = packed
-            cols = slice(first * P, (first + SLOTS_PER_GROUP) * P)
-            width = SLOTS_PER_GROUP * K_PASS
-            for g in range(PASSES):
-                nc.vector.quantize_mx(
-                    out=codes[:, g, cols].bitcast(FP8X4),
-                    scales=scales[:, g, cols],
-                    in_=group[:, g * width : (g + 1) * width],
-                )
+            which = first // SLOTS_PER_GROUP
+            nc.vector.quantize_mx(out=codes[:, which].bitcast(FP8X4), scales=scales[:, which], in_=group[:])
+
+        def weight_columns(packed, g, first, count):
+            group, column = divmod(first, SLOTS_PER_GROUP * P)
+            start = g * SLOTS_PER_GROUP * P + column
+            cols = slice(start, start + count)
+            return packed[0][:, group, cols].bitcast(FP8X4), packed[1][:, group, cols]
 
         x_bank, pk_bank, p_bank, product = {}, {}, {}, {}
         th, sq, d1, q, s_sum = {}, {}, {}, {}, {}
-        g_op, u_op, v_bank, o_bank, g_rows, u_rows = {}, {}, {}, {}, {}, {}
+        g_op, u_op, v_bank, o_bank = {}, {}, {}, {}
 
         def transpose_x(i):
             x_bank[i] = psum.tile([P, BANK], F32, tag="x", name="x_bank")
@@ -151,45 +150,15 @@ def tile_inimnetdisc_pa_kernel(tc, x, phi_j, phi_k, w_i, w_j, out):
 
         def tanh_x(i):
             th[i] = work.tile([P, D], F32, name="th")
-            if i < ROW_LAYOUT_TILES:
-                nc.scalar.activation(out=th[i][:], in_=x_sb[i][:], func=ACT.Tanh)
-            else:
-                nc.scalar.activation(out=packed_order(th[i][:]), in_=bank_in_packed_order(x_bank[i]), func=ACT.Tanh)
+            nc.scalar.activation(out=packed_order(th[i][:]), in_=bank_in_packed_order(x_bank[i]), func=ACT.Tanh)
 
         def square_t(i):
-            pool = keep if i < ROW_LAYOUT_TILES else work
-            sq[i] = pool.tile([P, D], F32, name="d1" if i < ROW_LAYOUT_TILES else "sq")
+            sq[i] = work.tile([P, D], F32, name="sq")
             nc.scalar.activation(out=sq[i][:], in_=th[i][:], func=ACT.Square)
 
         def slope(i):
             d1[i] = keep.tile([P, D], F32, name="d1")
             nc.scalar.activation(out=d1[i][:], in_=sq[i][:], func=ACT.Copy, scale=-1.0, bias=1.0)
-
-        def rows_fields(i):
-            product[i] = rowwork.tile([P, D], F32, name="row_product")
-            nc.vector.tensor_tensor(out=product[i][:], in0=pj_sb[i][:], in1=pk_sb[i][:], op=ALU.mult)
-
-        def rows_q(i):
-            q[i] = keep.tile([P, D], F32, name="q")
-            nc.vector.tensor_tensor(out=q[i][:], in0=th[i][:], in1=product[i][:], op=ALU.mult)
-
-        def rows_g(i):
-            g_rows[i] = rowwork.tile([P, D], BF16, name="g_rows")
-            nc.vector.scalar_tensor_tensor(
-                out=g_rows[i][:], in0=sq[i][:], scalar=1.0, in1=pk_sb[i][:], op0=ALU.subtract, op1=ALU.mult
-            )
-
-        def rows_u(i):
-            u_rows[i] = rowwork.tile([P, D], BF16, name="u_rows")
-            nc.vector.scalar_tensor_tensor(
-                out=u_rows[i][:], in0=sq[i][:], scalar=1.0, in1=s_sum[i][:], op0=ALU.subtract, op1=ALU.mult
-            )
-
-        def turn_rows(rows, tag, bf):
-            bank = psum.tile([P, BANK], F32, tag=tag, name="turn_bank")
-            transpose_rows(nc, bank, rows, ident)
-            words = bf.bitcast(F32).rearrange("p (g c h) -> p g c h", g=PASSES, h=HALVES)
-            nc.scalar.copy(out=words, in_=bank[:].rearrange("p (h g c) -> p g c h", h=HALVES, g=PASSES))
 
         def make_g(i, g_bf):
             nc.vector.tensor_tensor(
@@ -224,28 +193,14 @@ def tile_inimnetdisc_pa_kernel(tc, x, phi_j, phi_k, w_i, w_j, out):
         def first_product(i, g2):
             codes, scales, base = g_op[i]
             v_bank[i, g2] = psum.tile([P, BANK], F32, tag="v%d" % g2, name="v_bank")
-            if i < ROW_LAYOUT_TILES:
-                cols = slice(g2 * BANK, (g2 + 1) * BANK)
-                for g in range(PASSES):
-                    rows = slice(base + g * P, base + (g + 1) * P)
-                    nc.tensor.matmul_mx(
-                        out=v_bank[i, g2][:],
-                        lhsT=codes[:, rows].bitcast(FP8X4),
-                        lhsT_scale=scales[:, rows],
-                        rhs=wj[0][:, g, cols].bitcast(FP8X4),
-                        rhs_scale=wj[1][:, g, cols],
-                        start=(g == 0),
-                        stop=(g == PASSES - 1),
-                    )
-                return
             for t in range(PACK):
-                slot = slice((g2 * PACK + t) * P, (g2 * PACK + t + 1) * P)
                 for g in range(PASSES):
                     rows = slice(base + g * P, base + (g + 1) * P)
+                    w_codes, w_scales = weight_columns(wj, g, (g2 * PACK + t) * P, P)
                     nc.tensor.matmul_mx(
                         out=v_bank[i, g2][:, t * P : (t + 1) * P],
-                        lhsT=wj[0][:, g, slot].bitcast(FP8X4),
-                        lhsT_scale=wj[1][:, g, slot],
+                        lhsT=w_codes,
+                        lhsT_scale=w_scales,
                         rhs=codes[:, rows].bitcast(FP8X4),
                         rhs_scale=scales[:, rows],
                         start=(g == 0),
@@ -259,7 +214,7 @@ def tile_inimnetdisc_pa_kernel(tc, x, phi_j, phi_k, w_i, w_j, out):
             nc.vector.scalar_tensor_tensor(
                 out=s_sum[i][:, part].rearrange("p (r t) -> p r t", t=PACK),
                 in0=q[i][:, part].rearrange("p (r t) -> p r t", t=PACK),
-                scalar=2.0 if i < ROW_LAYOUT_TILES else -2.0,
+                scalar=-2.0,
                 in1=v_bank[i, g2][:].rearrange("p (t r) -> p r t", t=PACK),
                 op0=ALU.mult,
                 op1=ALU.add,
@@ -273,13 +228,13 @@ def tile_inimnetdisc_pa_kernel(tc, x, phi_j, phi_k, w_i, w_j, out):
             if g2 == 0 and (i, n) not in o_bank:
                 o_bank[i, n] = psum.tile([P, BANK], F32, tag=OUT_TAGS[(HALVES * i + n) % len(OUT_TAGS) if i > 3 else n], name="o_bank")
             rows = slice(g2 * P, (g2 + 1) * P)
-            cols = slice(n * BANK, (n + 1) * BANK)
+            w_codes, w_scales = weight_columns(wi, g2, n * BANK, BANK)
             nc.tensor.matmul_mx(
                 out=o_bank[i, n][:],
                 lhsT=codes[:, rows].bitcast(FP8X4),
                 lhsT_scale=scales[:, rows],
-                rhs=wi[0][:, g2, cols].bitcast(FP8X4),
-                rhs_scale=wi[1][:, g2, cols],
+                rhs=w_codes,
+                rhs_scale=w_scales,
                 start=(g2 == 0),
                 stop=(g2 == PASSES - 1),
             )
@@ -407,6 +362,8 @@ def tile_inimnetdisc_pa_kernel(tc, x, phi_j, phi_k, w_i, w_j, out):
                     transpose_x(i + 4)
                 for g in range(PASSES):
                     make_q(j, g)
+                    if g == 0 and i in (1, 2):
+                        quantise_slots(wi, groups[i - 1], (i - 1) * SLOTS_PER_GROUP)
                     if ahead:
                         transpose_product(ahead, g)
                 for late in now[1:]:
@@ -414,8 +371,6 @@ def tile_inimnetdisc_pa_kernel(tc, x, phi_j, phi_k, w_i, w_j, out):
                         second_half(late, n)
                         store_half(late, n, nc.scalar.copy)
                 quantise(pair, 0, 2 * D)
-                for group in {1: (0,), 2: (1,)}.get(i, ()):
-                    quantise_slots(wi, groups[group], group * SLOTS_PER_GROUP)
                 u_op[i] = pair[1][:, 0:WORDS], pair[2][:, 0:WORDS]
                 g_op[j] = pair[1], pair[2], WORDS
 

from contextlib import ExitStack

import concourse.mybir as mybir
from concourse.masks import make_identity

FLOPS = 2 * 2 * 1024 * 1024 * 1024

F32 = mybir.dt.float32
BF16 = mybir.dt.bfloat16
U32 = mybir.dt.uint32
U8 = mybir.dt.uint8
FP8X4 = mybir.dt.float8_e4m3fn_x4
ACT = mybir.ActivationFunctionType
ALU = mybir.AluOpType

P = 128
PACK = 4
K_PASS = P * PACK
ROWS = 1024
D = 1024
PASSES = D // K_PASS
ROW_TILES = ROWS // P
SLOTS = D // P
HALVES = 2
PAIR = 2
BANK = 512
WORDS = D // PACK
SLOTS_PER_GROUP = 4
WEIGHT_TAGS = ("v0", "v1", "o0", "o1")
OUT_TAGS = ("o0", "o1", "x", "pk", "p0", "p1")
FIELD_STEP = 2


def transpose_rows(nc, bank, rows, ident):
    words = rows.bitcast(F32)
    for g in range(PASSES):
        for h in range(HALVES):
            src = g * HALVES * P
            dst = (h * PASSES + g) * P
            nc.tensor.transpose(bank[:, dst : dst + P], words[:, src + h : src + HALVES * P : HALVES], ident[:])


def packed_order(flat):
    return flat.rearrange("p (c h e) -> p c h e", h=HALVES, e=PAIR)


def bank_in_packed_order(bank):
    return bank[:].bitcast(BF16).rearrange("p (h c e) -> p c h e", h=HALVES, e=PAIR)


def tile_inimnetdisc_pa_kernel(tc, x, phi_j, phi_k, w_i, w_j, out):
    nc = tc.nc
    with ExitStack() as ctx:
        const = ctx.enter_context(tc.tile_pool(name="const", bufs=1))
        inputs = ctx.enter_context(tc.tile_pool(name="inputs", bufs=1))
        weights = ctx.enter_context(tc.tile_pool(name="weights", bufs=1))
        wstage = ctx.enter_context(tc.tile_pool(name="wstage", bufs=2))
        work = ctx.enter_context(tc.tile_pool(name="work", bufs=2))
        keep = ctx.enter_context(tc.tile_pool(name="keep", bufs=4))
        products = ctx.enter_context(tc.tile_pool(name="products", bufs=2))
        mx = ctx.enter_context(tc.tile_pool(name="mx", bufs=3))
        results = ctx.enter_context(tc.tile_pool(name="results", bufs=7))
        psum = ctx.enter_context(tc.psum_pool(name="psum", bufs=1))

        x_rows = x.rearrange("(i p) d -> i p d", p=P)
        pj_rows = phi_j.rearrange("(i p) d -> i p d", p=P)
        pk_rows = phi_k.rearrange("(i p) d -> i p d", p=P)
        out_rows = out.rearrange("(i p) n -> i p n", p=P)
        wj_rows = w_j.rearrange("(g p h e) d -> g h p e d", p=P, h=HALVES, e=PAIR)
        wj_view = [wj_rows[g, h] for g in range(PASSES) for h in range(HALVES)]
        wi_rows = w_i.rearrange("(c e p) d -> c p e d", p=P, e=PAIR)
        wi_view = [wi_rows[c] for c in range(SLOTS // PAIR)]

        ident = const.tile([P, P], F32)
        make_identity(nc, ident[:])

        x_sb, pj_sb, pk_sb = {}, {}, {}
        sources = {"x": (x_sb, x_rows), "pk": (pk_sb, pk_rows), "pj": (pj_sb, pj_rows)}

        def load(i, what):
            tiles, rows = sources[what]
            tiles[i] = inputs.tile([P, D], BF16, name="%s%d" % (what, i))
            nc.sync.dma_start(out=tiles[i][:], in_=rows[i])

        def load_row_tile(i):
            for what in ("x", "pk", "pj"):
                load(i, what)

        def load_weight(view, name, c):
            raw = weights.tile([P, PAIR, D], BF16, name="%s_raw%d" % (name, c))
            nc.sync.dma_start(out=raw[:], in_=view[c])
            return raw

        def packed_weight(name):
            shape = [P, SLOTS // SLOTS_PER_GROUP, PASSES * SLOTS_PER_GROUP * P]
            codes = weights.tile(shape, U32, name="%s_codes" % name, align_bytes=64)
            scales = weights.tile(shape, U8, name="%s_scales" % name, align_bytes=64)
            return codes, scales

        def new_group():
            return wstage.tile([P, PASSES * SLOTS_PER_GROUP * K_PASS], BF16, name="group", align_bytes=64)

        def weight_slot(raw, group, slot, tag, copy):
            w_bank = psum.tile([P, BANK], F32, tag=tag, name="w_bank")
            transpose_rows(nc, w_bank, raw[slot // PAIR][:, slot % PAIR, :], ident)
            words = group[:].bitcast(F32)
            words = words.rearrange("p (g s c h) -> p g s c h", g=PASSES, s=SLOTS_PER_GROUP, h=HALVES)
            copy(out=words[:, :, slot % SLOTS_PER_GROUP, :, :], in_=w_bank[:].rearrange("p (h g c) -> p g c h", h=HALVES, g=PASSES))

        def quantise_slots(packed, group, first):
            codes, scales = packed
            which = first // SLOTS_PER_GROUP
            nc.vector.quantize_mx(out=codes[:, which].bitcast(FP8X4), scales=scales[:, which], in_=group[:])

        def weight_columns(packed, g, first, count):
            group, column = divmod(first, SLOTS_PER_GROUP * P)
            start = g * SLOTS_PER_GROUP * P + column
            cols = slice(start, start + count)
            return packed[0][:, group, cols].bitcast(FP8X4), packed[1][:, group, cols]

        x_bank, pk_bank, p_bank, product = {}, {}, {}, {}
        th, sq, d1, q, s_sum = {}, {}, {}, {}, {}
        g_op, u_op, v_bank, o_bank = {}, {}, {}, {}

        def transpose_x(i):
            x_bank[i] = psum.tile([P, BANK], F32, tag="x", name="x_bank")
            transpose_rows(nc, x_bank[i], x_sb[i][:], ident)

        def transpose_pk(i):
            pk_bank[i] = psum.tile([P, BANK], F32, tag="pk", name="pk_bank")
            transpose_rows(nc, pk_bank[i], pk_sb[i][:], ident)

        def multiply_fields(i):
            product[i] = products.tile([P, D], F32, name="product")
            for g in range(PASSES):
                part = slice(g * K_PASS, (g + 1) * K_PASS)
                dst = product[i][:, part].rearrange("r (t p) -> r t p", t=PACK)
                pj = pj_sb[i][:, part].rearrange("r (p t) -> r t p", t=PACK)
                pk = pk_sb[i][:, part].rearrange("r (p t) -> r t p", t=PACK)
                for t in range(0, PACK, FIELD_STEP):
                    some = slice(t, t + FIELD_STEP)
                    engine = nc.vector if i == 0 else nc.gpsimd
                    engine.tensor_tensor(out=dst[:, some], in0=pj[:, some], in1=pk[:, some], op=ALU.mult)

        def transpose_product(i, g):
            p_bank[i, g] = psum.tile([P, BANK], F32, tag="p%d" % g, name="p_bank")
            for t in range(PACK):
                src = g * K_PASS + t * P
                nc.tensor.transpose(p_bank[i, g][:, t * P : (t + 1) * P], product[i][:, src : src + P], ident[:])

        def tanh_x(i):
            th[i] = work.tile([P, D], F32, name="th")
            nc.scalar.activation(out=packed_order(th[i][:]), in_=bank_in_packed_order(x_bank[i]), func=ACT.Tanh)

        def square_t(i):
            sq[i] = work.tile([P, D], F32, name="sq")
            nc.scalar.activation(out=sq[i][:], in_=th[i][:], func=ACT.Square)

        def slope(i):
            d1[i] = keep.tile([P, D], F32, name="d1")
            nc.scalar.activation(out=d1[i][:], in_=sq[i][:], func=ACT.Copy, scale=-1.0, bias=1.0)

        def make_g(i, g_bf):
            nc.vector.tensor_tensor(
                out=packed_order(g_bf), in0=packed_order(d1[i][:]), in1=bank_in_packed_order(pk_bank[i]), op=ALU.mult
            )

        def make_q(i, g):
            if g == 0:
                q[i] = keep.tile([P, D], F32, name="q")
            part = slice(g * K_PASS, (g + 1) * K_PASS)
            nc.vector.tensor_tensor(
                out=q[i][:, part].rearrange("p (r t) -> p r t", t=PACK),
                in0=th[i][:, part].rearrange("p (r t) -> p r t", t=PACK),
                in1=p_bank[i, g][:].rearrange("p (t r) -> p r t", t=PACK),
                op=ALU.mult,
            )

        def new_operand(count):
            bf = mx.tile([P, count * D], BF16, tag="bf%d" % count, name="bf", align_bytes=64, bufs=count + 1)
            live = 2 if count == 1 else ROW_TILES - 2
            codes = mx.tile([P, count * WORDS], U32, tag="codes%d" % count, name="codes", align_bytes=64, bufs=live)
            scales = mx.tile([P, count * WORDS], U8, tag="scales%d" % count, name="scales", align_bytes=64, bufs=live)
            return bf, codes, scales

        def quantise(operand, first, count):
            bf, codes, scales = operand
            words = slice(first // PACK, (first + count) // PACK)
            nc.vector.quantize_mx(
                out=codes[:, words].bitcast(FP8X4), scales=scales[:, words], in_=bf[:, first : first + count]
            )

        def first_product(i, g2):
            codes, scales, base = g_op[i]
            v_bank[i, g2] = psum.tile([P, BANK], F32, tag="v%d" % g2, name="v_bank")
            for t in range(PACK):
                for g in range(PASSES):
                    rows = slice(base + g * P, base + (g + 1) * P)
                    w_codes, w_scales = weight_columns(wj, g, (g2 * PACK + t) * P, P)
                    nc.tensor.matmul_mx(
                        out=v_bank[i, g2][:, t * P : (t + 1) * P],
                        lhsT=w_codes,
                        lhsT_scale=w_scales,
                        rhs=codes[:, rows].bitcast(FP8X4),
                        rhs_scale=scales[:, rows],
                        start=(g == 0),
                        stop=(g == PASSES - 1),
                    )

        def add_v(i, g2):
            if g2 == 0:
                s_sum[i] = work.tile([P, D], F32, name="s_sum")
            part = slice(g2 * K_PASS, (g2 + 1) * K_PASS)
            nc.vector.scalar_tensor_tensor(
                out=s_sum[i][:, part].rearrange("p (r t) -> p r t", t=PACK),
                in0=q[i][:, part].rearrange("p (r t) -> p r t", t=PACK),
                scalar=-2.0,
                in1=v_bank[i, g2][:].rearrange("p (t r) -> p r t", t=PACK),
                op0=ALU.mult,
                op1=ALU.add,
            )

        def make_u(i, u_bf, part):
            nc.vector.tensor_tensor(out=u_bf[:, part], in0=s_sum[i][:, part], in1=d1[i][:, part], op=ALU.mult)

        def second_product(i, n, g2):
            codes, scales = u_op[i]
            if g2 == 0 and (i, n) not in o_bank:
                o_bank[i, n] = psum.tile([P, BANK], F32, tag=OUT_TAGS[(HALVES * i + n) % len(OUT_TAGS) if i > 3 else n], name="o_bank")
            rows = slice(g2 * P, (g2 + 1) * P)
            w_codes, w_scales = weight_columns(wi, g2, n * BANK, BANK)
            nc.tensor.matmul_mx(
                out=o_bank[i, n][:],
                lhsT=codes[:, rows].bitcast(FP8X4),
                lhsT_scale=scales[:, rows],
                rhs=w_codes,
                rhs_scale=w_scales,
                start=(g2 == 0),
                stop=(g2 == PASSES - 1),
            )

        def store_half(i, n, copy):
            cols = slice(n * BANK, (n + 1) * BANK)
            half = results.tile([P, BANK], F32, name="half")
            copy(out=half[:], in_=o_bank[i, n][:])
            nc.sync.dma_start(out=out_rows[i][:, cols], in_=half[:])

        def second_half(i, n):
            for g2 in range(PASSES):
                second_product(i, n, g2)

        def output_rows(i):
            for n in range(D // BANK):
                second_half(i, n)
                store_half(i, n, nc.scalar.copy)

        whole = slice(0, D)
        with tc.manual_schedule():
            wj_raw, wi_raw = [], []
            load_row_tile(0)
            load(1, "x")
            wj_raw += [load_weight(wj_view, "wj", 0), load_weight(wj_view, "wj", 1)]
            load(1, "pk")
            load(1, "pj")
            wj_raw += [load_weight(wj_view, "wj", 2), load_weight(wj_view, "wj", 3)]
            load_row_tile(2)
            load_row_tile(3)
            wi_raw += [load_weight(wi_view, "wi", c) for c in range(SLOTS // PAIR)]
            for i in range(4, ROW_TILES):
                load_row_tile(i)
            wj, wi = packed_weight("wj"), packed_weight("wi")

            first = new_operand(1), new_operand(1)
            group_a, group_b = new_group(), new_group()
            transpose_x(0)
            tanh_x(0)
            transpose_pk(0)
            multiply_fields(0)
            transpose_product(0, 0)
            transpose_product(0, 1)
            square_t(0)
            transpose_x(1)
            tanh_x(1)
            make_q(0, 0)
            make_q(0, 1)
            weight_slot(wj_raw, group_a, 0, WEIGHT_TAGS[0], nc.vector.tensor_copy)
            weight_slot(wj_raw, group_a, 1, WEIGHT_TAGS[1], nc.vector.tensor_copy)
            slope(0)
            square_t(1)
            slope(1)
            multiply_fields(1)
            weight_slot(wj_raw, group_a, 2, WEIGHT_TAGS[2], nc.vector.tensor_copy)
            weight_slot(wj_raw, group_a, 3, WEIGHT_TAGS[3], nc.vector.tensor_copy)
            make_g(0, first[0][0][:])
            quantise(first[0], 0, D)
            for slot in (4, 5):
                weight_slot(wj_raw, group_b, slot, WEIGHT_TAGS[slot % 4], nc.scalar.copy)
            quantise_slots(wj, group_a, 0)
            for slot in (6, 7):
                weight_slot(wj_raw, group_b, slot, WEIGHT_TAGS[slot % 4], nc.scalar.copy)
            transpose_pk(1)
            transpose_x(2)
            tanh_x(2)
            transpose_product(1, 0)
            transpose_product(1, 1)
            make_g(1, first[1][0][:])
            transpose_pk(2)
            transpose_x(3)
            multiply_fields(2)
            g_op[0] = first[0][1], first[0][2], 0
            g_op[1] = first[1][1], first[1][2], 0
            first_product(0, 0)
            make_q(1, 0)
            make_q(1, 1)
            square_t(2)
            quantise_slots(wj, group_b, 4)
            first_product(0, 1)
            quantise(first[1], 0, D)
            slope(2)
            transpose_product(2, 0)
            transpose_product(2, 1)

            outs = {3: (0,), 4: (1,), 5: (2, 3)}
            slots_of = {0: (0, 1, 2), 1: (3, 4, 5), 2: (6, 7)}
            groups = {}
            for i in range(ROW_TILES - 2):
                j = i + 2
                ahead = i + 3 if i + 3 < ROW_TILES else None
                slots = slots_of.get(i, ())
                now = outs.get(i, ())
                pair = new_operand(2)
                if ahead:
                    multiply_fields(ahead)
                    tanh_x(ahead)
                add_v(i, 0)
                add_v(i, 1)
                for s in slots[:2]:
                    if s % SLOTS_PER_GROUP == 0:
                        groups[s // SLOTS_PER_GROUP] = new_group()
                    weight_slot(wi_raw, groups[s // SLOTS_PER_GROUP], s, "o%d" % (s % 2), nc.scalar.copy)
                for late in now[:1]:
                    second_half(late, 0)
                    store_half(late, 0, nc.scalar.copy)
                if ahead:
                    square_t(ahead)
                first_product(i + 1, 0)
                first_product(i + 1, 1)
                if ahead:
                    slope(ahead)
                make_g(j, pair[0][:, D : 2 * D])
                make_u(i, pair[0], whole)
                if ahead:
                    transpose_pk(ahead)
                for s in slots[2:]:
                    if s % SLOTS_PER_GROUP == 0:
                        groups[s // SLOTS_PER_GROUP] = new_group()
                    weight_slot(wi_raw, groups[s // SLOTS_PER_GROUP], s, "o%d" % (s % 2), nc.scalar.copy)
                for late in now[:1]:
                    second_half(late, 1)
                    store_half(late, 1, nc.scalar.copy)
                if i + 4 < ROW_TILES:
                    transpose_x(i + 4)
                for g in range(PASSES):
                    make_q(j, g)
                    if g == 0 and i in (1, 2):
                        quantise_slots(wi, groups[i - 1], (i - 1) * SLOTS_PER_GROUP)
                    if ahead:
                        transpose_product(ahead, g)
                for late in now[1:]:
                    for n in range(D // BANK):
                        second_half(late, n)
                        store_half(late, n, nc.scalar.copy)
                quantise(pair, 0, 2 * D)
                u_op[i] = pair[1][:, 0:WORDS], pair[2][:, 0:WORDS]
                g_op[j] = pair[1], pair[2], WORDS

            i = ROW_TILES - 2
            add_v(i, 0)
            add_v(i, 1)
            first_product(i + 1, 0)
            first_product(i + 1, 1)
            output_rows(i - 2)
            u6 = new_operand(1)
            make_u(i, u6[0], whole)
            output_rows(i - 1)
            add_v(i + 1, 0)
            quantise(u6, 0, D)
            u_op[i] = u6[1], u6[2]
            add_v(i + 1, 1)
            output_rows(i)
            u7 = new_operand(1)
            for g2 in range(PASSES):
                make_u(i + 1, u7[0], slice(g2 * K_PASS, (g2 + 1) * K_PASS))
            u_op[i + 1] = u7[1], u7[2]
            for n in range(D // BANK):
                o_bank[i + 1, n] = psum.tile([P, BANK], F32, tag="v%d" % n, name="o_bank")
            for g2 in range(PASSES):
                quantise(u7, g2 * K_PASS, K_PASS)
                for n in range(D // BANK):
                    second_product(i + 1, n, g2)
            store_half(i + 1, 0, nc.scalar.copy)
            store_half(i + 1, 1, nc.vector.tensor_copy)
